import numpy as np
import ml_dtypes


def mxq(x, axis, fmt="e4m3"):
    dtype, down = {"e4m3": (ml_dtypes.float8_e4m3fn, 7), "e5m2": (ml_dtypes.float8_e5m2, 14)}[fmt]
    v = np.moveaxis(np.asarray(x, np.float32).astype(ml_dtypes.bfloat16).astype(np.float64), axis, -1)
    blocks = v.reshape(v.shape[:-1] + (-1, 32))
    amax = np.abs(blocks).max(-1, keepdims=True)
    byte = np.maximum(np.where(amax > 0, np.frexp(amax)[1] - 1 + 127, 0) - down, 1)
    scale = np.exp2(byte - 127.0)
    codes = (blocks / scale).astype(np.float32).astype(dtype).astype(np.float64)
    return np.moveaxis((codes * scale).reshape(v.shape), -1, axis)


WIDE = False


def mx_kscale(k):
    if not WIDE:
        return np.ones(k)
    levels = np.array([10, -10, 5, -5, 0])
    a = np.random.permutation(np.resize(levels, k // 512 * 4)).reshape(k // 512, 4)
    idx = np.arange(k)
    return np.exp2(a[idx // 512, idx % 128 // 32])


BF16 = ml_dtypes.bfloat16


def bf(x):
    return np.asarray(x, np.float32).astype(BF16)


def f64(x):
    return np.asarray(x).astype(np.float64)


E2M1 = np.array([0.0, 0.5, 1.0, 1.5, 2.0, 3.0, 4.0, 6.0, -0.0, -0.5, -1.0, -1.5, -2.0, -3.0, -4.0, -6.0])


def pack_weight(w, fmt):
    k, n = w.shape
    w = f64(bf(w)).reshape(k // 32, 32, n)
    amax = np.abs(w).max(1)
    if fmt == "e4m3":
        byte = np.frexp(amax)[1] - 1 + 127 - 7
    else:
        mant, ex = np.frexp(amax / 6.0)
        byte = np.where(mant > 0.5, ex, ex - 1) + 127
    byte = np.clip(np.where(amax > 0, byte, 1), 1, 254)
    scaled = (w * np.exp2(127.0 - byte)[:, None, :]).reshape(k, n).astype(np.float32)
    by_word = np.ascontiguousarray(scaled.reshape(k // 512, 128, 4, n).transpose(0, 1, 3, 2))
    if fmt == "e4m3":
        words = by_word.astype(ml_dtypes.float8_e4m3fn).view(np.uint8)
    else:
        c = by_word.astype(ml_dtypes.float4_e2m1fn).view(np.uint8) & 0xF
        words = c[..., 0::2] | (c[..., 1::2] << 4)
    return np.ascontiguousarray(words), np.ascontiguousarray(byte.astype(np.uint8).reshape(k // 512, 16, n))


def unpack_weight(words, scales, fmt):
    g, p, n, _ = words.shape
    if fmt == "e4m3":
        vals = np.ascontiguousarray(words).view(ml_dtypes.float8_e4m3fn).astype(np.float64)
    else:
        nib = np.empty((g, p, n, 4), np.uint8)
        nib[..., 0::2] = words & 0xF
        nib[..., 1::2] = words >> 4
        vals = E2M1[nib]
    vals = vals * np.repeat(np.exp2(scales.astype(np.float64) - 127.0), 8, axis=1)[..., None]
    return vals.transpose(0, 1, 3, 2).reshape(g * 512, n)

def pack4(w):
    words, scales = pack_weight(w, "e2m1")
    return words.reshape(words.shape[0], 128, -1), scales


def unpack4(words, scales):
    return unpack_weight(words.reshape(words.shape[0], 128, -1, 2), scales, "e2m1")


B, T, E, V, H, C = 1, 1024, 1024, 2048, 8, 512
KD = E // H
ROPE_BASE = 10000.0


def rotate_every_two(u):
    u1 = u[..., ::2]
    u2 = u[..., 1::2]
    return np.stack((-u2, u1), axis=-1).reshape(u.shape)


def theta_shift(u, sin, cos):
    return u * cos + rotate_every_two(u) * sin


def setup_inputs():
    s = mx_kscale(E)
    angle = np.arange(T)[:, None] * (1.0 / ROPE_BASE ** (np.repeat(np.arange(KD // 2), 2) * 2.0 / KD))
    x = bf(np.random.standard_normal((B, T, E)) * s)
    sin = bf(np.sin(angle))
    cos = bf(np.cos(angle))
    Wq_words, Wq_scales = pack4(np.random.standard_normal((E, E)) * 0.5 / np.sqrt(E) / s[:, None])
    Wk_words, Wk_scales = pack4(np.random.standard_normal((E, E)) * 2.0 / np.sqrt(E) / s[:, None])
    return {"x": x,
            "sin": sin, "cos": cos,
            "Wq_words": Wq_words, "Wq_scales": Wq_scales,
            "Wk_words": Wk_words, "Wk_scales": Wk_scales}


def reference(x, sin, cos, Wq_words, Wq_scales, Wk_words, Wk_scales):
    xq = mxq(f64(x), 2, "e4m3")
    q = (xq @ unpack4(Wq_words, Wq_scales)).reshape(B, T, H, KD).transpose(0, 2, 1, 3)
    k = ((xq @ unpack4(Wk_words, Wk_scales)) * KD ** -0.5).reshape(B, T, H, KD).transpose(0, 2, 1, 3)
    return theta_shift(q, f64(sin), f64(cos)), theta_shift(k, f64(sin), f64(cos))

@@ -1,0 +1,149 @@
+import concourse.mybir as mybir
+from concourse.masks import make_identity
+
+F32 = mybir.dt.float32
+BF16 = mybir.dt.bfloat16
+I32 = mybir.dt.int32
+U32 = mybir.dt.uint32
+U8 = mybir.dt.uint8
+FP8X4 = mybir.dt.float8_e4m3fn_x4
+FP4X4 = mybir.dt.float4_e2m1fn_x4
+MULT = mybir.AluOpType.mult
+ADD = mybir.AluOpType.add
+
+P = 128
+T = 1024
+E = 1024
+H = 8
+KD = E // H
+TILES = T // P
+PASSES = E // (4 * P)
+BANK = 512
+BANKS = E // BANK
+HEADS_PER_BANK = BANK // KD
+WEIGHTS = 2
+FACTOR = (1.0, KD**-0.5)
+
+FLOPS = 2 * T * E * WEIGHTS * E
+
+
+def tile_multiscaleretention_pa_kernel(
+    tc, x, sin, cos, Wq_words, Wq_scales, Wk_words, Wk_scales, out_0, out_1
+):
+    nc = tc.nc
+    x_tiles = x[0].rearrange("(p i) k -> i p k", i=TILES)
+    out_tiles = [o[0].rearrange("h (p i) c -> i p h c", i=TILES) for o in (out_0, out_1)]
+    given_words = (Wq_words, Wk_words)
+    given_scales = (Wq_scales, Wk_scales)
+
+    with tc.tile_pool(name="keep", bufs=1) as keep, tc.tile_pool(name="xin", bufs=TILES) as xin, tc.tile_pool(
+        name="stage", bufs=2
+    ) as stage, tc.tile_pool(name="rot", bufs=3) as rot, tc.psum_pool(name="flip", bufs=2) as flip, tc.psum_pool(
+        name="prod", bufs=6
+    ) as prod, tc.manual_schedule():
+        ident = keep.tile([P, P], F32)
+        w_words = keep.tile([P, WEIGHTS, PASSES, 2 * E], U8, align_bytes=64)
+        w_scales = keep.tile([P, WEIGHTS, PASSES, E], U8, align_bytes=64)
+        x_codes = keep.tile([P, TILES, PASSES * P], U32, align_bytes=64)
+        x_scales = keep.tile([P, TILES, PASSES * P], U8, align_bytes=64)
+        cos_sb = keep.tile([P, TILES, KD], BF16)
+        sin_sb = keep.tile([P, TILES, KD], BF16)
+        table_a = keep.tile([P, TILES, KD], BF16)
+        table_b = keep.tile([P, TILES, KD], BF16)
+
+        nc.vector.memset(w_scales[:].rearrange("p w g n -> p (w g n)").bitcast(I32), 0)
+        make_identity(nc, ident[:])
+
+        def load_x(i):
+            x_sb = xin.tile([P, E], BF16)
+            nc.sync.dma_start(out=x_sb[:], in_=x_tiles[i])
+            return x_sb
+
+        def load_weight(w):
+            by_quadrant = given_scales[w].rearrange("g (q r) n -> q r g n", r=4)
+            for q in range(4):
+                nc.sync.dma_start(
+                    out=w_scales[32 * q : 32 * q + 4, w, :, :].bitcast(I32), in_=by_quadrant[q].bitcast(I32)
+                )
+            for g in range(PASSES):
+                nc.sync.dma_start(out=w_words[:, w, g, :].bitcast(I32), in_=given_words[w][g].bitcast(I32))
+
+        x_sbs = [load_x(0)]
+        load_weight(0)
+        nc.sync.dma_start(out=cos_sb[:], in_=cos.rearrange("(p i) c -> p i c", i=TILES))
+        nc.sync.dma_start(out=sin_sb[:], in_=sin.rearrange("(p i) c -> p i c", i=TILES))
+        x_sbs.append(load_x(1))
+        load_weight(1)
+        for i in range(2, TILES):
+            x_sbs.append(load_x(i))
+
+        def prepare(i):
+            x_pairs = x_sbs[i][:].bitcast(F32)
+            flipped = flip.tile([P, PASSES * 2, P], F32)
+            for g in range(PASSES):
+                for u in range(2):
+                    nc.tensor.transpose(
+                        flipped[:, 2 * g + u, :], x_pairs[:, 256 * g + u : 256 * (g + 1) : 2], ident[:]
+                    )
+            grouped = stage.tile([P, PASSES, P, 4], BF16, align_bytes=64)
+            nc.scalar.copy(out=grouped[:].bitcast(F32), in_=flipped[:].rearrange("p (g u) r -> p g r u", u=2))
+            nc.scalar.copy(out=table_a[:, i, 0:KD:2], in_=cos_sb[:, i, 0:KD:2])
+            nc.scalar.copy(out=table_a[:, i, 1:KD:2], in_=sin_sb[:, i, 1:KD:2])
+            nc.scalar.mul(out=table_b[:, i, 0:KD:2], in_=sin_sb[:, i, 0:KD:2], mul=-1.0)
+            nc.scalar.copy(out=table_b[:, i, 1:KD:2], in_=cos_sb[:, i, 1:KD:2])
+            return grouped
+
+        def quantise(i, grouped):
+            nc.vector.quantize_mx(
+                out=x_codes[:, i, :].bitcast(FP8X4),
+                scales=x_scales[:, i, :],
+                in_=grouped[:].rearrange("p g r t -> p (g r t)"),
+            )
+
+        def project(i, w):
+            banks = []
+            for c in range(BANKS):
+                acc = prod.tile([P, BANK], F32)
+                for g in range(PASSES):
+                    nc.tensor.matmul_mx(
+                        out=acc[:],
+                        lhsT=x_codes[:, i, P * g : P * (g + 1)].bitcast(FP8X4),
+                        lhsT_scale=x_scales[:, i, P * g : P * (g + 1)],
+                        rhs=w_words[:, w, g, 2 * BANK * c : 2 * BANK * (c + 1)].bitcast(FP4X4),
+                        rhs_scale=w_scales[:, w, g, BANK * c : BANK * (c + 1)],
+                        start=(g == 0),
+                        stop=(g == PASSES - 1),
+                    )
+                banks.append(acc)
+            return banks
+
+        def rotate(i, w, banks):
+            shape = [P, HEADS_PER_BANK, KD // 2, 2]
+            by_pair = "p (h n e) -> p h n e"
+            part_a = rot.tile([P, E], F32)
+            part_b = rot.tile([P, E], F32)
+            for c in range(BANKS):
+                cols = slice(BANK * c, BANK * (c + 1))
+                u = banks[c][:].rearrange(by_pair, h=HEADS_PER_BANK, e=2)
+                for e, table, part in ((0, table_a, part_a), (1, table_b, part_b)):
+                    nc.vector.scalar_tensor_tensor(
+                        out=part[:, cols].rearrange(by_pair, h=HEADS_PER_BANK, e=2),
+                        in0=u[:, :, :, e : e + 1].to_broadcast(shape),
+                        scalar=FACTOR[w],
+                        in1=table[:, i, :].rearrange("p (n e) -> p n e", e=2).unsqueeze(1).to_broadcast(shape),
+                        op0=MULT,
+                        op1=MULT,
+                    )
+            rotated = rot.tile([P, E], F32)
+            nc.gpsimd.tensor_tensor(out=rotated[:], in0=part_a[:], in1=part_b[:], op=ADD)
+            nc.sync.dma_start(out=out_tiles[w][i], in_=rotated[:].rearrange("p (h c) -> p h c", h=H))
+
+        quantise(0, prepare(0))
+        for n in range(TILES * WEIGHTS):
+            i, w = divmod(n, WEIGHTS)
+            banks = project(i, w)
+            if n + 1 < TILES:
+                grouped = prepare(n + 1)
+            rotate(i, w, banks)
+            if n + 1 < TILES:
+                quantise(n + 1, grouped)

@@ -31,13 +31,15 @@ def tile_multiscaleretention_pa_kernel(
     tc, x, sin, cos, Wq_words, Wq_scales, Wk_words, Wk_scales, out_0, out_1
 ):
     nc = tc.nc
-    x_tiles = x[0].rearrange("(p i) k -> i p k", i=TILES)
-    out_tiles = [o[0].rearrange("h (p i) c -> i p h c", i=TILES) for o in (out_0, out_1)]
+    x_tiles = x[0].rearrange("(i p) k -> i p k", p=P)
+    cos_tiles = cos.rearrange("(i p) c -> i p c", p=P)
+    sin_tiles = sin.rearrange("(i p) c -> i p c", p=P)
+    out_tiles = [o[0].rearrange("h (i p) c -> i p h c", p=P) for o in (out_0, out_1)]
     given_words = (Wq_words, Wk_words)
     given_scales = (Wq_scales, Wk_scales)
 
     with tc.tile_pool(name="keep", bufs=1) as keep, tc.tile_pool(name="xin", bufs=TILES) as xin, tc.tile_pool(
-        name="stage", bufs=2
+        name="stage", bufs=4
     ) as stage, tc.tile_pool(name="rot", bufs=3) as rot, tc.psum_pool(name="flip", bufs=2) as flip, tc.psum_pool(
         name="prod", bufs=6
     ) as prod, tc.manual_schedule():
@@ -54,9 +56,11 @@ def tile_multiscaleretention_pa_kernel(
         nc.vector.memset(w_scales[:].rearrange("p w g n -> p (w g n)").bitcast(I32), 0)
         make_identity(nc, ident[:])
 
-        def load_x(i):
+        def load_tile(i):
             x_sb = xin.tile([P, E], BF16)
             nc.sync.dma_start(out=x_sb[:], in_=x_tiles[i])
+            nc.sync.dma_start(out=cos_sb[:, i, :], in_=cos_tiles[i])
+            nc.sync.dma_start(out=sin_sb[:, i, :], in_=sin_tiles[i])
             return x_sb
 
         def load_weight(w):
@@ -65,40 +69,40 @@ def tile_multiscaleretention_pa_kernel(
                 nc.sync.dma_start(
                     out=w_scales[32 * q : 32 * q + 4, w, :, :].bitcast(I32), in_=by_quadrant[q].bitcast(I32)
                 )
-            for g in range(PASSES):
-                nc.sync.dma_start(out=w_words[:, w, g, :].bitcast(I32), in_=given_words[w][g].bitcast(I32))
+            nc.sync.dma_start(
+                out=w_words[:, w, :, :].bitcast(I32), in_=given_words[w].rearrange("g p n -> p g n").bitcast(I32)
+            )
 
-        x_sbs = [load_x(0)]
+        x_sbs = [load_tile(0)]
         load_weight(0)
-        nc.sync.dma_start(out=cos_sb[:], in_=cos.rearrange("(p i) c -> p i c", i=TILES))
-        nc.sync.dma_start(out=sin_sb[:], in_=sin.rearrange("(p i) c -> p i c", i=TILES))
-        x_sbs.append(load_x(1))
+        x_sbs.append(load_tile(1))
         load_weight(1)
         for i in range(2, TILES):
-            x_sbs.append(load_x(i))
+            x_sbs.append(load_tile(i))
 
         def prepare(i):
             x_pairs = x_sbs[i][:].bitcast(F32)
-            flipped = flip.tile([P, PASSES * 2, P], F32)
+            by_pass = []
             for g in range(PASSES):
+                flipped = flip.tile([P, 2, P], F32)
                 for u in range(2):
-                    nc.tensor.transpose(
-                        flipped[:, 2 * g + u, :], x_pairs[:, 256 * g + u : 256 * (g + 1) : 2], ident[:]
-                    )
-            grouped = stage.tile([P, PASSES, P, 4], BF16, align_bytes=64)
-            nc.scalar.copy(out=grouped[:].bitcast(F32), in_=flipped[:].rearrange("p (g u) r -> p g r u", u=2))
+                    nc.tensor.transpose(flipped[:, u, :], x_pairs[:, 256 * g + u : 256 * (g + 1) : 2], ident[:])
+                grouped = stage.tile([P, P, 4], BF16, align_bytes=64)
+                nc.scalar.copy(out=grouped[:].bitcast(F32), in_=flipped[:].rearrange("p u r -> p r u"))
+                by_pass.append(grouped)
             nc.scalar.copy(out=table_a[:, i, 0:KD:2], in_=cos_sb[:, i, 0:KD:2])
             nc.scalar.copy(out=table_a[:, i, 1:KD:2], in_=sin_sb[:, i, 1:KD:2])
             nc.scalar.mul(out=table_b[:, i, 0:KD:2], in_=sin_sb[:, i, 0:KD:2], mul=-1.0)
             nc.scalar.copy(out=table_b[:, i, 1:KD:2], in_=cos_sb[:, i, 1:KD:2])
-            return grouped
+            return by_pass
 
-        def quantise(i, grouped):
-            nc.vector.quantize_mx(
-                out=x_codes[:, i, :].bitcast(FP8X4),
-                scales=x_scales[:, i, :],
-                in_=grouped[:].rearrange("p g r t -> p (g r t)"),
-            )
+        def quantise(i, by_pass):
+            for g in range(PASSES):
+                nc.vector.quantize_mx(
+                    out=x_codes[:, i, P * g : P * (g + 1)].bitcast(FP8X4),
+                    scales=x_scales[:, i, P * g : P * (g + 1)],
+                    in_=by_pass[g][:].rearrange("p r t -> p (r t)"),
+                )
 
         def project(i, w):
             banks = []
@@ -117,7 +121,7 @@ def tile_multiscaleretention_pa_kernel(
                 banks.append(acc)
             return banks
 
-        def rotate(i, w, banks):
+        def rotate(i, w, banks, last):
             shape = [P, HEADS_PER_BANK, KD // 2, 2]
             by_pair = "p (h n e) -> p h n e"
             part_a = rot.tile([P, E], F32)
@@ -135,15 +139,21 @@ def tile_multiscaleretention_pa_kernel(
                         op1=MULT,
                     )
             rotated = rot.tile([P, E], F32)
-            nc.gpsimd.tensor_tensor(out=rotated[:], in0=part_a[:], in1=part_b[:], op=ADD)
-            nc.sync.dma_start(out=out_tiles[w][i], in_=rotated[:].rearrange("p (h c) -> p h c", h=H))
+            engine, pieces = (nc.vector, BANKS) if last else (nc.gpsimd, 1)
+            for piece in range(pieces):
+                cols = slice(E // pieces * piece, E // pieces * (piece + 1))
+                heads = slice(H // pieces * piece, H // pieces * (piece + 1))
+                engine.tensor_tensor(out=rotated[:, cols], in0=part_a[:, cols], in1=part_b[:, cols], op=ADD)
+                nc.sync.dma_start(
+                    out=out_tiles[w][i][:, heads, :], in_=rotated[:, cols].rearrange("p (h c) -> p h c", c=KD)
+                )
 
         quantise(0, prepare(0))
         for n in range(TILES * WEIGHTS):
             i, w = divmod(n, WEIGHTS)
             banks = project(i, w)
             if n + 1 < TILES:
-                grouped = prepare(n + 1)
-            rotate(i, w, banks)
+                by_pass = prepare(n + 1)
+            rotate(i, w, banks, last=(n == TILES * WEIGHTS - 1))
             if n + 1 < TILES:
-                quantise(n + 1, grouped)
+                quantise(n + 1, by_pass)

@@ -69,9 +69,10 @@ def tile_multiscaleretention_pa_kernel(
                 nc.sync.dma_start(
                     out=w_scales[32 * q : 32 * q + 4, w, :, :].bitcast(I32), in_=by_quadrant[q].bitcast(I32)
                 )
-            nc.sync.dma_start(
-                out=w_words[:, w, :, :].bitcast(I32), in_=given_words[w].rearrange("g p n -> p g n").bitcast(I32)
-            )
+            by_partition = given_words[w].rearrange("g p n -> p g n")
+            for c in range(BANKS):
+                half = slice(2 * BANK * c, 2 * BANK * (c + 1))
+                nc.sync.dma_start(out=w_words[:, w, :, half].bitcast(I32), in_=by_partition[:, :, half].bitcast(I32))
 
         x_sbs = [load_tile(0)]
         load_weight(0)
@@ -121,7 +122,7 @@ def tile_multiscaleretention_pa_kernel(
                 banks.append(acc)
             return banks
 
-        def rotate(i, w, banks, last):
+        def rotate(i, w, banks, units_left):
             shape = [P, HEADS_PER_BANK, KD // 2, 2]
             by_pair = "p (h n e) -> p h n e"
             part_a = rot.tile([P, E], F32)
@@ -139,7 +140,8 @@ def tile_multiscaleretention_pa_kernel(
                         op1=MULT,
                     )
             rotated = rot.tile([P, E], F32)
-            engine, pieces = (nc.vector, BANKS) if last else (nc.gpsimd, 1)
+            engine = nc.vector if units_left == 0 else nc.gpsimd
+            pieces = BANKS if units_left <= 1 else 1
             for piece in range(pieces):
                 cols = slice(E // pieces * piece, E // pieces * (piece + 1))
                 heads = slice(H // pieces * piece, H // pieces * (piece + 1))
@@ -154,6 +156,6 @@ def tile_multiscaleretention_pa_kernel(
             banks = project(i, w)
             if n + 1 < TILES:
                 by_pass = prepare(n + 1)
-            rotate(i, w, banks, last=(n == TILES * WEIGHTS - 1))
+            rotate(i, w, banks, units_left=TILES * WEIGHTS - 1 - n)
             if n + 1 < TILES:
                 quantise(n + 1, by_pass)

@@ -32,15 +32,15 @@ def tile_multiscaleretention_pa_kernel(
 ):
     nc = tc.nc
     x_tiles = x[0].rearrange("(i p) k -> i p k", p=P)
-    cos_tiles = cos.rearrange("(i p) c -> i p c", p=P)
-    sin_tiles = sin.rearrange("(i p) c -> i p c", p=P)
+    cos_tiles = cos.rearrange("(i p) c -> p i c", p=P)
+    sin_tiles = sin.rearrange("(i p) c -> p i c", p=P)
     out_tiles = [o[0].rearrange("h (i p) c -> i p h c", p=P) for o in (out_0, out_1)]
     given_words = (Wq_words, Wk_words)
     given_scales = (Wq_scales, Wk_scales)
 
     with tc.tile_pool(name="keep", bufs=1) as keep, tc.tile_pool(name="xin", bufs=TILES) as xin, tc.tile_pool(
         name="stage", bufs=4
-    ) as stage, tc.tile_pool(name="rot", bufs=3) as rot, tc.psum_pool(name="flip", bufs=2) as flip, tc.psum_pool(
+    ) as stage, tc.tile_pool(name="rot", bufs=3) as rot, tc.tile_pool(name="turn", bufs=3) as turn, tc.psum_pool(name="flip", bufs=2) as flip, tc.psum_pool(
         name="prod", bufs=6
     ) as prod, tc.manual_schedule():
         ident = keep.tile([P, P], F32)
@@ -53,109 +53,215 @@ def tile_multiscaleretention_pa_kernel(
         table_a = keep.tile([P, TILES, KD], BF16)
         table_b = keep.tile([P, TILES, KD], BF16)
 
-        nc.vector.memset(w_scales[:].rearrange("p w g n -> p (w g n)").bitcast(I32), 0)
+        for w in range(WEIGHTS):
+            nc.vector.memset(w_scales[:, w, :, :].rearrange("p g n -> p (g n)").bitcast(I32), 0)
+        ident_bf = keep.tile([P, P], BF16)
+        swap = keep.tile([P, P], F32)
+        cross_sb = keep.tile([P, KD], BF16)
+        tables_t = keep.tile([P, 2, P], BF16)
+        warm = keep.tile([P, BANK], BF16)
+        nc.gpsimd.memset(warm[:].bitcast(F32), 0.0)
         make_identity(nc, ident[:])
+        make_identity(nc, ident_bf[:])
+        nc.gpsimd.tensor_copy(out=swap[:, 0:P:2], in_=ident[:, 1:P:2])
+        nc.gpsimd.tensor_copy(out=swap[:, 1:P:2], in_=ident[:, 0:P:2])
 
         def load_tile(i):
             x_sb = xin.tile([P, E], BF16)
             nc.sync.dma_start(out=x_sb[:], in_=x_tiles[i])
-            nc.sync.dma_start(out=cos_sb[:, i, :], in_=cos_tiles[i])
-            nc.sync.dma_start(out=sin_sb[:, i, :], in_=sin_tiles[i])
             return x_sb
 
-        def load_weight(w):
+        def load_tables(lo, hi):
+            nc.sync.dma_start(out=cos_sb[:, lo:hi, :], in_=cos_tiles[:, lo:hi, :])
+            nc.sync.dma_start(out=sin_sb[:, lo:hi, :], in_=sin_tiles[:, lo:hi, :])
+
+        def load_scales(w):
             by_quadrant = given_scales[w].rearrange("g (q r) n -> q r g n", r=4)
             for q in range(4):
                 nc.sync.dma_start(
                     out=w_scales[32 * q : 32 * q + 4, w, :, :].bitcast(I32), in_=by_quadrant[q].bitcast(I32)
                 )
-            by_partition = given_words[w].rearrange("g p n -> p g n")
-            for c in range(BANKS):
-                half = slice(2 * BANK * c, 2 * BANK * (c + 1))
-                nc.sync.dma_start(out=w_words[:, w, :, half].bitcast(I32), in_=by_partition[:, :, half].bitcast(I32))
+
+        def load_words(w, c):
+            half = slice(2 * BANK * c, 2 * BANK * (c + 1))
+            nc.sync.dma_start(
+                out=w_words[:, w, :, half].bitcast(I32),
+                in_=given_words[w].rearrange("g p n -> p g n")[:, :, half].bitcast(I32),
+            )
 
         x_sbs = [load_tile(0)]
-        load_weight(0)
+        load_words(0, 0)
+        load_tables(0, 2)
+        load_scales(0)
+        load_words(0, 1)
         x_sbs.append(load_tile(1))
-        load_weight(1)
-        for i in range(2, TILES):
+        load_scales(1)
+        load_words(1, 0)
+        load_words(1, 1)
+        x_sbs.append(load_tile(2))
+        load_tables(2, TILES)
+        for i in range(3, TILES):
             x_sbs.append(load_tile(i))
 
         def prepare(i):
             x_pairs = x_sbs[i][:].bitcast(F32)
-            by_pass = []
+            grouped = stage.tile([P, PASSES, P, 4], BF16, align_bytes=64)
             for g in range(PASSES):
-                flipped = flip.tile([P, 2, P], F32)
+                bank = flip.tile([P, BANK], F32)
+                flipped = bank[:, 0 : 2 * P].rearrange("p (u r) -> p u r", u=2)
                 for u in range(2):
                     nc.tensor.transpose(flipped[:, u, :], x_pairs[:, 256 * g + u : 256 * (g + 1) : 2], ident[:])
-                grouped = stage.tile([P, P, 4], BF16, align_bytes=64)
-                nc.scalar.copy(out=grouped[:].bitcast(F32), in_=flipped[:].rearrange("p u r -> p r u"))
-                by_pass.append(grouped)
+                nc.scalar.copy(out=grouped[:, g, :, :].bitcast(F32), in_=flipped.rearrange("p u r -> p r u"))
             nc.scalar.copy(out=table_a[:, i, 0:KD:2], in_=cos_sb[:, i, 0:KD:2])
             nc.scalar.copy(out=table_a[:, i, 1:KD:2], in_=sin_sb[:, i, 1:KD:2])
             nc.scalar.mul(out=table_b[:, i, 0:KD:2], in_=sin_sb[:, i, 0:KD:2], mul=-1.0)
             nc.scalar.copy(out=table_b[:, i, 1:KD:2], in_=cos_sb[:, i, 1:KD:2])
-            return by_pass
+            return grouped
 
-        def quantise(i, by_pass):
-            for g in range(PASSES):
+        def quantise(i, grouped):
+            pieces = PASSES if i == 0 else 1
+            for piece in range(pieces):
+                words = slice(PASSES * P // pieces * piece, PASSES * P // pieces * (piece + 1))
                 nc.vector.quantize_mx(
-                    out=x_codes[:, i, P * g : P * (g + 1)].bitcast(FP8X4),
-                    scales=x_scales[:, i, P * g : P * (g + 1)],
-                    in_=by_pass[g][:].rearrange("p r t -> p (r t)"),
+                    out=x_codes[:, i, words].bitcast(FP8X4),
+                    scales=x_scales[:, i, words],
+                    in_=grouped[:].rearrange("p g r t -> p (g r t)")[:, 4 * words.start : 4 * words.stop],
                 )
 
-        def project(i, w):
-            banks = []
-            for c in range(BANKS):
-                acc = prod.tile([P, BANK], F32)
+        def project(i, w, c):
+            acc = prod.tile([P, BANK], F32)
+            for g in range(PASSES):
+                nc.tensor.matmul_mx(
+                    out=acc[:],
+                    lhsT=x_codes[:, i, P * g : P * (g + 1)].bitcast(FP8X4),
+                    lhsT_scale=x_scales[:, i, P * g : P * (g + 1)],
+                    rhs=w_words[:, w, g, 2 * BANK * c : 2 * BANK * (c + 1)].bitcast(FP4X4),
+                    rhs_scale=w_scales[:, w, g, BANK * c : BANK * (c + 1)],
+                    start=(g == 0),
+                    stop=(g == PASSES - 1),
+                )
+            return acc
+
+        def project_t(i, w, c):
+            acc = prod.tile([P, BANK], F32, name="acc")
+            for j in range(HEADS_PER_BANK):
+                h = HEADS_PER_BANK * c + j
                 for g in range(PASSES):
                     nc.tensor.matmul_mx(
-                        out=acc[:],
-                        lhsT=x_codes[:, i, P * g : P * (g + 1)].bitcast(FP8X4),
-                        lhsT_scale=x_scales[:, i, P * g : P * (g + 1)],
-                        rhs=w_words[:, w, g, 2 * BANK * c : 2 * BANK * (c + 1)].bitcast(FP4X4),
-                        rhs_scale=w_scales[:, w, g, BANK * c : BANK * (c + 1)],
+                        out=acc[:, P * j : P * (j + 1)],
+                        lhsT=w_words[:, w, g, 2 * KD * h : 2 * KD * (h + 1)].bitcast(FP4X4),
+                        lhsT_scale=w_scales[:, w, g, KD * h : KD * (h + 1)],
+                        rhs=x_codes[:, i, P * g : P * (g + 1)].bitcast(FP8X4),
+                        rhs_scale=x_scales[:, i, P * g : P * (g + 1)],
                         start=(g == 0),
                         stop=(g == PASSES - 1),
                     )
-                banks.append(acc)
-            return banks
+            return acc
 
-        def rotate(i, w, banks, units_left):
+        def turn_tables(i):
+            nc.scalar.copy(out=cross_sb[:, 0:KD:2], in_=sin_sb[:, i, 1:KD:2])
+            nc.scalar.mul(out=cross_sb[:, 1:KD:2], in_=sin_sb[:, i, 0:KD:2], mul=-1.0)
+            bank = flip.tile([P, BANK], F32, name="bank")
+            turned = bank[:].bitcast(BF16)[:, 0 : 2 * P]
+            nc.tensor.transpose(turned[:, 0:P], cos_sb[:, i, :], ident_bf[:])
+            nc.tensor.transpose(turned[:, P : 2 * P], cross_sb[:], ident_bf[:])
+            nc.scalar.copy(out=tables_t[:].rearrange("p a r -> p (a r)"), in_=turned)
+
+        def rotate_t(w, acc):
+            turn_a = turn.tile([P, BANK], F32)
+            turn_b = turn.tile([P, BANK], F32)
+            for a, part in ((0, turn_a), (1, turn_b)):
+                nc.vector.scalar_tensor_tensor(
+                    out=part[:].rearrange("p (h r) -> p h r", r=P),
+                    in0=acc[:].rearrange("p (h r) -> p h r", r=P),
+                    scalar=FACTOR[w],
+                    in1=tables_t[:, a, :].unsqueeze(1).to_broadcast([P, HEADS_PER_BANK, P]),
+                    op0=MULT,
+                    op1=MULT,
+                )
+            return turn_a, turn_b
+
+        def add_t(i, w, c, sides):
+            bank = flip.tile([P, BANK], F32, name="bank")
+            for j in range(HEADS_PER_BANK):
+                cols = slice(P * j, P * (j + 1))
+                nc.tensor.matmul(
+                    out=bank[:, cols], lhsT=sides[0][:, cols], rhs=ident[:], start=True, stop=False, is_transpose=True
+                )
+                nc.tensor.matmul(
+                    out=bank[:, cols], lhsT=sides[1][:, cols], rhs=swap[:], start=False, stop=True, is_transpose=True
+                )
+            turned = turn.tile([P, BANK], F32)
+            nc.scalar.copy(out=turned[:], in_=bank[:])
+            store(i, w, HEADS_PER_BANK * c, turned[:])
+
+        def store(i, w, h, source):
+            heads = slice(h, h + source.shape[1] // KD)
+            nc.sync.dma_start(out=out_tiles[w][i][:, heads, :], in_=source.rearrange("p (h c) -> p h c", c=KD))
+
+        def multiply(i, w, acc, part_a, part_b):
             shape = [P, HEADS_PER_BANK, KD // 2, 2]
             by_pair = "p (h n e) -> p h n e"
-            part_a = rot.tile([P, E], F32)
-            part_b = rot.tile([P, E], F32)
-            for c in range(BANKS):
-                cols = slice(BANK * c, BANK * (c + 1))
-                u = banks[c][:].rearrange(by_pair, h=HEADS_PER_BANK, e=2)
-                for e, table, part in ((0, table_a, part_a), (1, table_b, part_b)):
-                    nc.vector.scalar_tensor_tensor(
-                        out=part[:, cols].rearrange(by_pair, h=HEADS_PER_BANK, e=2),
-                        in0=u[:, :, :, e : e + 1].to_broadcast(shape),
-                        scalar=FACTOR[w],
-                        in1=table[:, i, :].rearrange("p (n e) -> p n e", e=2).unsqueeze(1).to_broadcast(shape),
-                        op0=MULT,
-                        op1=MULT,
-                    )
-            rotated = rot.tile([P, E], F32)
-            engine = nc.vector if units_left == 0 else nc.gpsimd
-            pieces = BANKS if units_left <= 1 else 1
-            for piece in range(pieces):
-                cols = slice(E // pieces * piece, E // pieces * (piece + 1))
-                heads = slice(H // pieces * piece, H // pieces * (piece + 1))
-                engine.tensor_tensor(out=rotated[:, cols], in0=part_a[:, cols], in1=part_b[:, cols], op=ADD)
-                nc.sync.dma_start(
-                    out=out_tiles[w][i][:, heads, :], in_=rotated[:, cols].rearrange("p (h c) -> p h c", c=KD)
+            u = acc[:].rearrange(by_pair, h=HEADS_PER_BANK, e=2)
+            for e, table, part in ((0, table_a, part_a), (1, table_b, part_b)):
+                nc.vector.scalar_tensor_tensor(
+                    out=part.rearrange(by_pair, h=HEADS_PER_BANK, e=2),
+                    in0=u[:, :, :, e : e + 1].to_broadcast(shape),
+                    scalar=FACTOR[w],
+                    in1=table[:, i, :].rearrange("p (n e) -> p n e", e=2).unsqueeze(1).to_broadcast(shape),
+                    op0=MULT,
+                    op1=MULT,
                 )
 
-        quantise(0, prepare(0))
-        for n in range(TILES * WEIGHTS):
+        def add(engine, i, w, h, part_a, part_b, rotated):
+            engine.tensor_tensor(out=rotated, in0=part_a, in1=part_b, op=ADD)
+            store(i, w, h, rotated)
+
+        def warm_up(count):
+            spare = prod.tile([P, BANK], F32, name="acc")
+            for k in range(count):
+                nc.tensor.matmul(out=spare[:], lhsT=warm[:, 0:P], rhs=warm[:], start=True, stop=True)
+
+        warm_up(3)
+        by_pass = prepare(0)
+        warm_up(2)
+        quantise(0, by_pass)
+        for n in range(TILES * WEIGHTS - WEIGHTS):
             i, w = divmod(n, WEIGHTS)
-            banks = project(i, w)
+            accs = [project(i, w, c) for c in range(BANKS)]
             if n + 1 < TILES:
                 by_pass = prepare(n + 1)
-            rotate(i, w, banks, units_left=TILES * WEIGHTS - 1 - n)
+            if n == TILES + 1:
+                turn_tables(TILES - 1)
+            part_a = rot.tile([P, E], F32)
+            part_b = rot.tile([P, E], F32)
+            rotated = rot.tile([P, E], F32)
+            by_bank = n == TILES * WEIGHTS - WEIGHTS - 1
+            for c in range(BANKS):
+                cols = slice(BANK * c, BANK * (c + 1))
+                multiply(i, w, accs[c], part_a[:, cols], part_b[:, cols])
+                if by_bank:
+                    add(nc.gpsimd, i, w, HEADS_PER_BANK * c, part_a[:, cols], part_b[:, cols], rotated[:, cols])
+            if not by_bank:
+                add(nc.gpsimd, i, w, 0, part_a[:], part_b[:], rotated[:])
             if n + 1 < TILES:
                 quantise(n + 1, by_pass)
+
+        i = TILES - 1
+        acc_q1 = project_t(i, 0, 1)
+        acc_q0 = project_t(i, 0, 0)
+        acc_k0 = project_t(i, 1, 0)
+        acc_k1 = project(i, 1, 1)
+        sides = rotate_t(0, acc_q1)
+        add_t(i, 0, 1, sides)
+        sides = rotate_t(0, acc_q0)
+        add_t(i, 0, 0, sides)
+        part_a = rot.tile([P, E], F32)
+        part_b = rot.tile([P, E], F32)
+        rotated = rot.tile([P, E], F32)
+        sides = rotate_t(1, acc_k0)
+        add_t(i, 1, 0, sides)
+        multiply(i, 1, acc_k1, part_a[:, BANK:E], part_b[:, BANK:E])
+        for h in range(0, HEADS_PER_BANK, 2):
+            cols = slice(BANK + KD * h, BANK + KD * (h + 2))
+            add(nc.vector, i, 1, HEADS_PER_BANK + h, part_a[:, cols], part_b[:, cols], rotated[:, cols])

import concourse.mybir as mybir
from concourse.masks import make_identity

F32 = mybir.dt.float32
BF16 = mybir.dt.bfloat16
I32 = mybir.dt.int32
U32 = mybir.dt.uint32
U8 = mybir.dt.uint8
FP8X4 = mybir.dt.float8_e4m3fn_x4
FP4X4 = mybir.dt.float4_e2m1fn_x4
MULT = mybir.AluOpType.mult
ADD = mybir.AluOpType.add

P = 128
T = 1024
E = 1024
H = 8
KD = E // H
TILES = T // P
PASSES = E // (4 * P)
BANK = 512
BANKS = E // BANK
HEADS_PER_BANK = BANK // KD
WEIGHTS = 2
FACTOR = (1.0, KD**-0.5)

FLOPS = 2 * T * E * WEIGHTS * E


def tile_multiscaleretention_pa_kernel(
    tc, x, sin, cos, Wq_words, Wq_scales, Wk_words, Wk_scales, out_0, out_1
):
    nc = tc.nc
    x_tiles = x[0].rearrange("(i p) k -> i p k", p=P)
    cos_tiles = cos.rearrange("(i p) c -> p i c", p=P)
    sin_tiles = sin.rearrange("(i p) c -> p i c", p=P)
    out_tiles = [o[0].rearrange("h (i p) c -> i p h c", p=P) for o in (out_0, out_1)]
    given_words = (Wq_words, Wk_words)
    given_scales = (Wq_scales, Wk_scales)

    with tc.tile_pool(name="keep", bufs=1) as keep, tc.tile_pool(name="xin", bufs=TILES) as xin, tc.tile_pool(
        name="stage", bufs=4
    ) as stage, tc.tile_pool(name="rot", bufs=3) as rot, tc.tile_pool(name="turn", bufs=3) as turn, tc.psum_pool(name="flip", bufs=2) as flip, tc.psum_pool(
        name="prod", bufs=6
    ) as prod, tc.manual_schedule():
        ident = keep.tile([P, P], F32)
        w_words = keep.tile([P, WEIGHTS, PASSES, 2 * E], U8, align_bytes=64)
        w_scales = keep.tile([P, WEIGHTS, PASSES, E], U8, align_bytes=64)
        x_codes = keep.tile([P, TILES, PASSES * P], U32, align_bytes=64)
        x_scales = keep.tile([P, TILES, PASSES * P], U8, align_bytes=64)
        cos_sb = keep.tile([P, TILES, KD], BF16)
        sin_sb = keep.tile([P, TILES, KD], BF16)
        table_a = keep.tile([P, TILES, KD], BF16)
        table_b = keep.tile([P, TILES, KD], BF16)

        for w in range(WEIGHTS):
            nc.vector.memset(w_scales[:, w, :, :].rearrange("p g n -> p (g n)").bitcast(I32), 0)
        ident_bf = keep.tile([P, P], BF16)
        swap = keep.tile([P, P], F32)
        cross_sb = keep.tile([P, KD], BF16)
        tables_t = keep.tile([P, 2, P], BF16)
        warm = keep.tile([P, BANK], BF16)
        nc.gpsimd.memset(warm[:].bitcast(F32), 0.0)
        make_identity(nc, ident[:])
        make_identity(nc, ident_bf[:])
        nc.gpsimd.tensor_copy(out=swap[:, 0:P:2], in_=ident[:, 1:P:2])
        nc.gpsimd.tensor_copy(out=swap[:, 1:P:2], in_=ident[:, 0:P:2])

        def load_tile(i):
            x_sb = xin.tile([P, E], BF16)
            nc.sync.dma_start(out=x_sb[:], in_=x_tiles[i])
            return x_sb

        def load_tables(lo, hi):
            nc.sync.dma_start(out=cos_sb[:, lo:hi, :], in_=cos_tiles[:, lo:hi, :])
            nc.sync.dma_start(out=sin_sb[:, lo:hi, :], in_=sin_tiles[:, lo:hi, :])

        def load_scales(w):
            by_quadrant = given_scales[w].rearrange("g (q r) n -> q r g n", r=4)
            for q in range(4):
                nc.sync.dma_start(
                    out=w_scales[32 * q : 32 * q + 4, w, :, :].bitcast(I32), in_=by_quadrant[q].bitcast(I32)
                )

        def load_words(w, c):
            half = slice(2 * BANK * c, 2 * BANK * (c + 1))
            nc.sync.dma_start(
                out=w_words[:, w, :, half].bitcast(I32),
                in_=given_words[w].rearrange("g p n -> p g n")[:, :, half].bitcast(I32),
            )

        x_sbs = [load_tile(0)]
        load_words(0, 0)
        load_tables(0, 2)
        load_scales(0)
        load_words(0, 1)
        x_sbs.append(load_tile(1))
        load_scales(1)
        load_words(1, 0)
        load_words(1, 1)
        x_sbs.append(load_tile(2))
        load_tables(2, TILES)
        for i in range(3, TILES):
            x_sbs.append(load_tile(i))

        def prepare(i):
            x_pairs = x_sbs[i][:].bitcast(F32)
            grouped = stage.tile([P, PASSES, P, 4], BF16, align_bytes=64)
            for g in range(PASSES):
                bank = flip.tile([P, BANK], F32)
                flipped = bank[:, 0 : 2 * P].rearrange("p (u r) -> p u r", u=2)
                for u in range(2):
                    nc.tensor.transpose(flipped[:, u, :], x_pairs[:, 256 * g + u : 256 * (g + 1) : 2], ident[:])
                nc.scalar.copy(out=grouped[:, g, :, :].bitcast(F32), in_=flipped.rearrange("p u r -> p r u"))
            nc.scalar.copy(out=table_a[:, i, 0:KD:2], in_=cos_sb[:, i, 0:KD:2])
            nc.scalar.copy(out=table_a[:, i, 1:KD:2], in_=sin_sb[:, i, 1:KD:2])
            nc.scalar.mul(out=table_b[:, i, 0:KD:2], in_=sin_sb[:, i, 0:KD:2], mul=-1.0)
            nc.scalar.copy(out=table_b[:, i, 1:KD:2], in_=cos_sb[:, i, 1:KD:2])
            return grouped

        def quantise(i, grouped):
            pieces = PASSES if i == 0 else 1
            for piece in range(pieces):
                words = slice(PASSES * P // pieces * piece, PASSES * P // pieces * (piece + 1))
                nc.vector.quantize_mx(
                    out=x_codes[:, i, words].bitcast(FP8X4),
                    scales=x_scales[:, i, words],
                    in_=grouped[:].rearrange("p g r t -> p (g r t)")[:, 4 * words.start : 4 * words.stop],
                )

        def project(i, w, c):
            acc = prod.tile([P, BANK], F32)
            for g in range(PASSES):
                nc.tensor.matmul_mx(
                    out=acc[:],
                    lhsT=x_codes[:, i, P * g : P * (g + 1)].bitcast(FP8X4),
                    lhsT_scale=x_scales[:, i, P * g : P * (g + 1)],
                    rhs=w_words[:, w, g, 2 * BANK * c : 2 * BANK * (c + 1)].bitcast(FP4X4),
                    rhs_scale=w_scales[:, w, g, BANK * c : BANK * (c + 1)],
                    start=(g == 0),
                    stop=(g == PASSES - 1),
                )
            return acc

        def project_t(i, w, c):
            acc = prod.tile([P, BANK], F32, name="acc")
            for j in range(HEADS_PER_BANK):
                h = HEADS_PER_BANK * c + j
                for g in range(PASSES):
                    nc.tensor.matmul_mx(
                        out=acc[:, P * j : P * (j + 1)],
                        lhsT=w_words[:, w, g, 2 * KD * h : 2 * KD * (h + 1)].bitcast(FP4X4),
                        lhsT_scale=w_scales[:, w, g, KD * h : KD * (h + 1)],
                        rhs=x_codes[:, i, P * g : P * (g + 1)].bitcast(FP8X4),
                        rhs_scale=x_scales[:, i, P * g : P * (g + 1)],
                        start=(g == 0),
                        stop=(g == PASSES - 1),
                    )
            return acc

        def turn_tables(i):
            nc.scalar.copy(out=cross_sb[:, 0:KD:2], in_=sin_sb[:, i, 1:KD:2])
            nc.scalar.mul(out=cross_sb[:, 1:KD:2], in_=sin_sb[:, i, 0:KD:2], mul=-1.0)
            bank = flip.tile([P, BANK], F32, name="bank")
            turned = bank[:].bitcast(BF16)[:, 0 : 2 * P]
            nc.tensor.transpose(turned[:, 0:P], cos_sb[:, i, :], ident_bf[:])
            nc.tensor.transpose(turned[:, P : 2 * P], cross_sb[:], ident_bf[:])
            nc.scalar.copy(out=tables_t[:].rearrange("p a r -> p (a r)"), in_=turned)

        def rotate_t(w, acc):
            turn_a = turn.tile([P, BANK], F32)
            turn_b = turn.tile([P, BANK], F32)
            for a, part in ((0, turn_a), (1, turn_b)):
                nc.vector.scalar_tensor_tensor(
                    out=part[:].rearrange("p (h r) -> p h r", r=P),
                    in0=acc[:].rearrange("p (h r) -> p h r", r=P),
                    scalar=FACTOR[w],
                    in1=tables_t[:, a, :].unsqueeze(1).to_broadcast([P, HEADS_PER_BANK, P]),
                    op0=MULT,
                    op1=MULT,
                )
            return turn_a, turn_b

        def add_t(i, w, c, sides):
            bank = flip.tile([P, BANK], F32, name="bank")
            for j in range(HEADS_PER_BANK):
                cols = slice(P * j, P * (j + 1))
                nc.tensor.matmul(
                    out=bank[:, cols], lhsT=sides[0][:, cols], rhs=ident[:], start=True, stop=False, is_transpose=True
                )
                nc.tensor.matmul(
                    out=bank[:, cols], lhsT=sides[1][:, cols], rhs=swap[:], start=False, stop=True, is_transpose=True
                )
            turned = turn.tile([P, BANK], F32)
            nc.scalar.copy(out=turned[:], in_=bank[:])
            store(i, w, HEADS_PER_BANK * c, turned[:])

        def store(i, w, h, source):
            heads = slice(h, h + source.shape[1] // KD)
            nc.sync.dma_start(out=out_tiles[w][i][:, heads, :], in_=source.rearrange("p (h c) -> p h c", c=KD))

        def multiply(i, w, acc, part_a, part_b):
            shape = [P, HEADS_PER_BANK, KD // 2, 2]
            by_pair = "p (h n e) -> p h n e"
            u = acc[:].rearrange(by_pair, h=HEADS_PER_BANK, e=2)
            for e, table, part in ((0, table_a, part_a), (1, table_b, part_b)):
                nc.vector.scalar_tensor_tensor(
                    out=part.rearrange(by_pair, h=HEADS_PER_BANK, e=2),
                    in0=u[:, :, :, e : e + 1].to_broadcast(shape),
                    scalar=FACTOR[w],
                    in1=table[:, i, :].rearrange("p (n e) -> p n e", e=2).unsqueeze(1).to_broadcast(shape),
                    op0=MULT,
                    op1=MULT,
                )

        def add(engine, i, w, h, part_a, part_b, rotated):
            engine.tensor_tensor(out=rotated, in0=part_a, in1=part_b, op=ADD)
            store(i, w, h, rotated)

        def warm_up(count):
            spare = prod.tile([P, BANK], F32, name="acc")
            for k in range(count):
                nc.tensor.matmul(out=spare[:], lhsT=warm[:, 0:P], rhs=warm[:], start=True, stop=True)

        warm_up(3)
        by_pass = prepare(0)
        warm_up(2)
        quantise(0, by_pass)
        for n in range(TILES * WEIGHTS - WEIGHTS):
            i, w = divmod(n, WEIGHTS)
            accs = [project(i, w, c) for c in range(BANKS)]
            if n + 1 < TILES:
                by_pass = prepare(n + 1)
            if n == TILES + 1:
                turn_tables(TILES - 1)
            part_a = rot.tile([P, E], F32)
            part_b = rot.tile([P, E], F32)
            rotated = rot.tile([P, E], F32)
            by_bank = n == TILES * WEIGHTS - WEIGHTS - 1
            for c in range(BANKS):
                cols = slice(BANK * c, BANK * (c + 1))
                multiply(i, w, accs[c], part_a[:, cols], part_b[:, cols])
                if by_bank:
                    add(nc.gpsimd, i, w, HEADS_PER_BANK * c, part_a[:, cols], part_b[:, cols], rotated[:, cols])
            if not by_bank:
                add(nc.gpsimd, i, w, 0, part_a[:], part_b[:], rotated[:])
            if n + 1 < TILES:
                quantise(n + 1, by_pass)

        i = TILES - 1
        acc_q1 = project_t(i, 0, 1)
        acc_q0 = project_t(i, 0, 0)
        acc_k0 = project_t(i, 1, 0)
        acc_k1 = project(i, 1, 1)
        sides = rotate_t(0, acc_q1)
        add_t(i, 0, 1, sides)
        sides = rotate_t(0, acc_q0)
        add_t(i, 0, 0, sides)
        part_a = rot.tile([P, E], F32)
        part_b = rot.tile([P, E], F32)
        rotated = rot.tile([P, E], F32)
        sides = rotate_t(1, acc_k0)
        add_t(i, 1, 0, sides)
        multiply(i, 1, acc_k1, part_a[:, BANK:E], part_b[:, BANK:E])
        for h in range(0, HEADS_PER_BANK, 2):
            cols = slice(BANK + KD * h, BANK + KD * (h + 2))
            add(nc.vector, i, 1, HEADS_PER_BANK + h, part_a[:, cols], part_b[:, cols], rotated[:, cols])
